import numpy as np
import ml_dtypes


def mxq(x, axis, fmt="e4m3"):
    dtype, down = {"e4m3": (ml_dtypes.float8_e4m3fn, 7), "e5m2": (ml_dtypes.float8_e5m2, 14)}[fmt]
    v = np.moveaxis(np.asarray(x, np.float32).astype(ml_dtypes.bfloat16).astype(np.float64), axis, -1)
    blocks = v.reshape(v.shape[:-1] + (-1, 32))
    amax = np.abs(blocks).max(-1, keepdims=True)
    byte = np.maximum(np.where(amax > 0, np.frexp(amax)[1] - 1 + 127, 0) - down, 1)
    scale = np.exp2(byte - 127.0)
    codes = (blocks / scale).astype(np.float32).astype(dtype).astype(np.float64)
    return np.moveaxis((codes * scale).reshape(v.shape), -1, axis)


WIDE = False


def mx_kscale(k):
    if not WIDE:
        return np.ones(k)
    levels = np.array([10, -10, 5, -5, 0])
    if k % 512:
        return np.exp2(np.random.permutation(np.resize(levels, k // 32))).repeat(32)
    a = np.empty((k // 512, 16))
    for p in range(k // 512):
        a[p, :8] = np.random.permutation(np.resize(levels, 8))
        for g in range(8):
            far = levels[np.abs(levels - a[p, g]) >= 10]
            a[p, g + 8] = far[np.random.randint(len(far))]
    return np.exp2(a.ravel()).repeat(32)


BF16 = ml_dtypes.bfloat16


def bf(x):
    return np.asarray(x, np.float32).astype(BF16)


def f64(x):
    return np.asarray(x).astype(np.float64)


B, HD, NH, H, W, F = 2, 1024, 8, 16, 32, 2048
HEAD = HD // NH
P = H * W


def rms_in(x, w, eps=1e-8):
    std = np.std(x, axis=(-2, -1), keepdims=True, ddof=1)
    return x / (std + eps) * w[None, :, None, None]


def setup_inputs():
    n = np.random.standard_normal
    s = mx_kscale(HD)

    def stream():
        return n((B, NH, H, W, HEAD)) * 0.35 * (0.5 + np.random.random((B, NH, 1, 1, HEAD))) + 0.5 * n((B, NH, 1, 1, HEAD))

    return {"xx": bf(stream()), "xy": bf(stream()),
            "x": bf(n((B, HD, H, W)) * (0.5 + np.random.random((B, HD, 1, 1))) + 0.5 * n((B, HD, 1, 1))),
            "norm2_w": bf((1.0 + 0.1 * n(HD)) * s),
            "out_w": bf(n((HD, HD)) / np.sqrt(HD) / s[None, :]),
            "out_b": bf(0.1 * n(HD)),
            "gamma_att": bf(0.5 + 0.2 * n(HD))}


def reference(xx, xy, x, norm2_w, out_w, out_b, gamma_att):
    a = (f64(xx) + f64(xy)) * 0.5
    a = a.transpose(0, 1, 4, 2, 3).reshape(B, HD, H, W)
    a = rms_in(a, f64(norm2_w)).reshape(B, HD, P)
    a = (mxq(f64(out_w), 1, "e4m3") @ mxq(a, 1, "e4m3")) + f64(out_b)[None, :, None]
    return a.reshape(B, HD, H, W) * f64(gamma_att)[None, :, None, None] + f64(x)

@@ -1,0 +1,334 @@
+from contextlib import ExitStack
+
+import concourse.mybir as mybir
+from concourse.masks import make_identity
+
+FLOPS = 2 * 1024 * 1024 * 1024
+
+F32 = mybir.dt.float32
+BF16 = mybir.dt.bfloat16
+U32 = mybir.dt.uint32
+U8 = mybir.dt.uint8
+FP8X4 = mybir.dt.float8_e4m3fn_x4
+ACT = mybir.ActivationFunctionType
+ALU = mybir.AluOpType
+AXIS = mybir.AxisListType
+
+P = 128
+POSITIONS = 512
+CHUNKS = 4
+HEADS = 4
+QUADS = 32
+PACK = 4
+PASSES = 4
+ROW_TILES = 8
+MEAN_COLUMNS = 2
+
+
+def tile_axialattentionblock_pb_kernel(tc, xx, xy, x, norm2_w, out_w, out_b, gamma_att, out):
+    nc = tc.nc
+    with ExitStack() as ctx:
+        const = ctx.enter_context(tc.tile_pool(name="const", bufs=1))
+        inputs = ctx.enter_context(tc.tile_pool(name="inputs", bufs=1))
+        keep = ctx.enter_context(tc.tile_pool(name="keep", bufs=1))
+        sums = ctx.enter_context(tc.tile_pool(name="sums", bufs=2))
+        stage = ctx.enter_context(tc.tile_pool(name="stage", bufs=2))
+        small = ctx.enter_context(tc.tile_pool(name="small", bufs=4))
+        ps_heads = ctx.enter_context(tc.psum_pool(name="ps_heads", bufs=4))
+        ps_weights = ctx.enter_context(tc.psum_pool(name="ps_weights", bufs=2))
+        ps_products = ctx.enter_context(tc.psum_pool(name="ps_products", bufs=2))
+        ctx.enter_context(tc.manual_schedule())
+
+        weight_bf = const.tile([P, 2, PACK], BF16, name="weight_bf")
+        gamma_bf = const.tile([P, ROW_TILES], BF16, name="gamma_bf")
+        bias_bf = const.tile([P, ROW_TILES], BF16, name="bias_bf")
+        with nc.allow_non_contiguous_dma(reason="three vectors of 1,024 values, eight values to a partition"):
+            nc.scalar.dma_start(out=weight_bf[:], in_=norm2_w.rearrange("(g p t) -> p g t", g=2, t=PACK))
+            nc.scalar.dma_start(out=gamma_bf[:], in_=gamma_att.rearrange("(p m) -> p m", m=ROW_TILES))
+            nc.scalar.dma_start(out=bias_bf[:], in_=out_b.rearrange("(p m) -> p m", m=ROW_TILES))
+
+        xx_sb = []
+        xy_sb = []
+        w_sb = []
+        x_sb = []
+
+        def load_pair(k, by_head):
+            b, n0 = k // 4, 2 * (k % 4)
+            tiles = []
+            for name, tiles_of in (("xx", xx_sb), ("xy", xy_sb)):
+                t = inputs.tile([P, 2, POSITIONS], BF16, name="%s_%d" % (name, k))
+                tiles_of.append(t)
+                tiles.append(t)
+            if by_head:
+                for j in range(2):
+                    for src, t in zip((xx, xy), tiles):
+                        nc.sync.dma_start(
+                            out=t[:, j, :], in_=src[b, n0 + j].rearrange("h (q r) c -> (h q) (r c)", r=CHUNKS))
+            else:
+                for src, t in zip((xx, xy), tiles):
+                    nc.sync.dma_start(
+                        out=t[:], in_=src[b, n0:n0 + 2].rearrange("n h (q r) c -> (h q) n (r c)", r=CHUNKS))
+
+        def load_weights(i):
+            t = inputs.tile([P, 2, 1024], BF16, name="w_sb%d" % i)
+            nc.sync.dma_start(out=t[:], in_=out_w.rearrange("(p m) j -> p m j", m=ROW_TILES)[:, 2 * i:2 * i + 2, :])
+            w_sb.append(t)
+
+        def load_residual(b):
+            t = inputs.tile([P, ROW_TILES, POSITIONS], BF16, name="x_sb%d" % b)
+            nc.sync.dma_start(out=t[:], in_=x[b].rearrange("(p m) h w -> p m (h w)", m=ROW_TILES))
+            x_sb.append(t)
+
+        one = const.tile([P, 1], F32, name="one")
+        nc.vector.memset(one[:], 1.0)
+        warm = const.tile([P, 1], F32, name="warm")
+        nc.scalar.activation(out=warm[:], in_=one[:], func=ACT.Sqrt)
+        minus_mean_weight = const.tile([P, MEAN_COLUMNS], BF16, name="minus_mean_weight")
+        nc.vector.memset(minus_mean_weight[:], -1.0 / POSITIONS)
+        ident = const.tile([P, P], F32, name="ident")
+        make_identity(nc, ident[:])
+
+        load_pair(0, True)
+        for k in (1, 2, 3):
+            load_pair(k, False)
+        load_weights(0)
+        load_weights(1)
+        load_pair(4, False)
+        load_pair(5, False)
+        load_weights(2)
+        load_weights(3)
+        load_pair(6, False)
+        load_residual(0)
+        load_pair(7, False)
+        load_residual(1)
+
+        same_quad = const.tile([P, QUADS], F32, name="same_quad")
+        nc.vector.tensor_reduce(out=same_quad[:], in_=ident[:].rearrange("c (q t) -> c q t", t=PACK), axis=AXIS.X, op=ALU.add)
+        same_slot = const.tile([P, PACK], F32, name="same_slot")
+        nc.vector.tensor_reduce(out=same_slot[:], in_=ident[:].rearrange("c (q t) -> c t q", t=PACK), axis=AXIS.X, op=ALU.add)
+        half_w = const.tile([P, 2, PACK], F32, name="half_w")
+        gamma = const.tile([P, ROW_TILES], F32, name="gamma")
+        gamma_bias = const.tile([P, ROW_TILES], F32, name="gamma_bias")
+
+        head_mean = {}
+        minus_mean = {}
+        summed = {}
+        slot_ps = {}
+        square_sum = {}
+        deviation = {}
+        factor = {}
+        scaled = {}
+        grouped = {}
+        g_codes = {}
+        g_scales = {}
+
+        def sum_positions(u):
+            t = ps_products.tile([P, HEADS, MEAN_COLUMNS], F32, name="mean_ps", tag="products")
+            for n in range(HEADS):
+                k, j = 2 * u + n // 2, n % 2
+                blocks = [src[k][:, j, P * r:P * r + P] for src in (xx_sb, xy_sb) for r in range(CHUNKS)]
+                for i, block in enumerate(blocks):
+                    nc.tensor.matmul(t[:, n, :], lhsT=block, rhs=minus_mean_weight[:],
+                                     start=(i == 0), stop=(i == len(blocks) - 1))
+            head_mean[u] = t
+
+        def add_streams(u):
+            s = sums.tile([P, CHUNKS, PACK, HEADS, QUADS], F32, name="summed")
+            for n in range(HEADS):
+                k, j = 2 * u + n // 2, n % 2
+                a, b = [src[k][:, j, :].rearrange("p (r q t) -> p r t q", r=CHUNKS, t=PACK) for src in (xx_sb, xy_sb)]
+                nc.vector.tensor_tensor(out=s[:, :, :, n, :], in0=a, in1=b, op=ALU.add)
+            summed[u] = s
+
+        def move_means(u):
+            spread = small.tile([P, HEADS, QUADS], F32, name="spread")
+            nc.vector.tensor_tensor(
+                out=spread[:], in0=same_quad[:].unsqueeze(1).to_broadcast([P, HEADS, QUADS]),
+                in1=head_mean[u][:, :, 0:1].to_broadcast([P, HEADS, QUADS]), op=ALU.mult)
+            moved = ps_products.tile([P, PACK], F32, name="moved", tag="products")
+            nc.tensor.matmul(moved[:], lhsT=spread[:].rearrange("p n q -> p (n q)"), rhs=same_slot[:], start=True, stop=True)
+            t = small.tile([P, PACK], F32, name="minus_mean")
+            nc.vector.tensor_copy(out=t[:], in_=moved[:])
+            minus_mean[u] = t
+
+        def transpose_slot(u, t):
+            bank = ps_heads.tile([P, POSITIONS], F32, name="slot_ps", tag="heads")
+            for r in range(CHUNKS):
+                nc.tensor.transpose(bank[:, P * r:P * r + P], summed[u][:, r, t, :, :].rearrange("p n q -> p (n q)"), ident[:])
+            slot_ps[(u, t)] = bank
+
+        def deviations(u):
+            sq = small.tile([P, PACK], F32, name="square_sum")
+            for t in range(PACK):
+                unused = small.tile([P, POSITIONS], BF16, name="unused")
+                nc.scalar.activation(out=unused[:], in_=slot_ps[(u, t)][:], func=ACT.Square,
+                                     bias=minus_mean[u][:, t:t + 1], scale=1.0, accum_out=sq[:, t:t + 1])
+            square_sum[u] = sq
+            d = small.tile([P, PACK], F32, name="deviation")
+            nc.scalar.activation(out=d[:], in_=sq[:], func=ACT.Sqrt, scale=1.0 / (4.0 * (POSITIONS - 1)))
+            deviation[u] = d
+
+        def factors(u):
+            denominator = small.tile([P, PACK], F32, name="denominator")
+            nc.vector.tensor_scalar(out=denominator[:], in0=deviation[u][:], scalar1=1e-8, scalar2=None, op0=ALU.add)
+            inverse = small.tile([P, PACK], F32, name="inverse")
+            nc.vector.reciprocal(out=inverse[:], in_=denominator[:])
+            f = small.tile([P, PACK], F32, name="factor")
+            nc.vector.tensor_tensor(out=f[:], in0=inverse[:], in1=half_w[:, u % 2, :], op=ALU.mult)
+            factor[u] = f
+
+        def scale_slot(u, t):
+            if t == 0:
+                fresh = stage.tile([P, PACK, POSITIONS], BF16, name="scaled")
+                scaled[u] = fresh
+            nc.scalar.activation(
+                out=scaled[u][:, t, :].rearrange("c (p r) -> c p r", r=CHUNKS),
+                in_=slot_ps[(u, t)][:].rearrange("c (r p) -> c p r", r=CHUNKS),
+                func=ACT.Copy, scale=factor[u][:, t:t + 1])
+
+        def regroup(u):
+            t = stage.tile([P, POSITIONS, PACK], BF16, name="grouped", align_bytes=64)
+            nc.vector.tensor_copy(out=t[:].rearrange("p (c i) t -> p c t i", i=4),
+                                  in_=scaled[u][:].rearrange("p t (c i) -> p c t i", i=4))
+            grouped[u] = t
+
+        def quantise_stream(u):
+            codes = keep.tile([P, POSITIONS], U32, name="g_codes%d" % u, align_bytes=64)
+            scales = keep.tile([P, POSITIONS], U8, name="g_scales%d" % u, align_bytes=64)
+            nc.vector.quantize_mx(out=codes[:].bitcast(FP8X4), scales=scales[:],
+                                  in_=grouped[u][:].rearrange("p w t -> p (w t)"))
+            g_codes[u] = codes
+            g_scales[u] = scales
+
+        w_ps = {}
+        w_grouped = {}
+        w_codes = {}
+        w_scales = {}
+
+        def transpose_weights(m):
+            bank = ps_weights.tile([P, 2, 2, P], F32, name="w_ps", tag="w_ps")
+            words = w_sb[m // 2][:, m % 2, :].bitcast(F32)
+            for g in range(2):
+                for h in range(2):
+                    nc.tensor.transpose(bank[:, g, h, :], words[:, 256 * g + h:256 * g + 256:2], ident[:])
+            w_ps[m] = bank
+
+        def copy_weights(m):
+            i = m % 2
+            if i == 0:
+                fresh = stage.tile([P, 2, 2, P, PACK], BF16, name="w_grouped", align_bytes=64)
+                w_grouped[m // 2] = fresh
+            dst = w_grouped[m // 2][:, i].bitcast(F32)
+            src = w_ps[m][:].rearrange("p g h o -> p g o h")
+            if i == 0:
+                nc.scalar.copy(out=dst, in_=src)
+            else:
+                nc.vector.tensor_copy(out=dst, in_=src)
+
+        def quantise_weights(i):
+            codes = keep.tile([P, 4, P], U32, name="w_codes%d" % i, align_bytes=64)
+            scales = keep.tile([P, 4, P], U8, name="w_scales%d" % i, align_bytes=64)
+            nc.vector.quantize_mx(out=codes[:].rearrange("p a o -> p (a o)").bitcast(FP8X4),
+                                  scales=scales[:].rearrange("p a o -> p (a o)"),
+                                  in_=w_grouped[i][:].rearrange("p i g o t -> p (i g o t)"))
+            w_codes[i] = codes
+            w_scales[i] = scales
+
+        result = {}
+        product = {}
+
+        def residual(b, m):
+            if m % 2 == 0:
+                fresh = keep.tile([P, 2, POSITIONS], F32, name="result%d%d" % (b, m // 2))
+                result[(b, m // 2)] = fresh
+            dst = result[(b, m // 2)][:, m % 2, :]
+            if b == 0:
+                nc.vector.tensor_scalar(out=dst, in0=x_sb[b][:, m, :], scalar1=1.0, scalar2=gamma_bias[:, m:m + 1],
+                                        op0=ALU.mult, op1=ALU.add)
+            else:
+                nc.scalar.activation(out=dst, in_=x_sb[b][:, m, :], func=ACT.Identity,
+                                     bias=gamma_bias[:, m:m + 1], scale=1.0)
+
+        def multiply(b, m):
+            if b == 0:
+                t = ps_products.tile([P, POSITIONS], F32, name="product", tag="products")
+            else:
+                t = ps_heads.tile([P, POSITIONS], F32, name="product", tag="heads")
+            for g in range(2):
+                nc.tensor.matmul_mx(
+                    out=t[:],
+                    lhsT=w_codes[m // 2][:, 2 * (m % 2) + g, :].bitcast(FP8X4),
+                    lhsT_scale=w_scales[m // 2][:, 2 * (m % 2) + g, :],
+                    rhs=g_codes[2 * b + g][:].bitcast(FP8X4),
+                    rhs_scale=g_scales[2 * b + g][:],
+                    start=(g == 0), stop=(g == 1))
+            product[(b, m)] = t
+
+        def finish(b, m):
+            t = result[(b, m // 2)]
+            nc.vector.scalar_tensor_tensor(out=t[:, m % 2, :], in0=product[(b, m)][:], scalar=gamma[:, m:m + 1],
+                                           in1=t[:, m % 2, :], op0=ALU.mult, op1=ALU.add)
+            view = out[b].rearrange("(p m) h w -> p m (h w)", m=ROW_TILES)
+            if b == 1:
+                nc.sync.dma_start(out=view[:, m, :], in_=t[:, m % 2, :])
+            elif m % 2 == 1:
+                nc.sync.dma_start(out=view[:, m - 1:m + 1, :], in_=t[:])
+
+        nc.vector.tensor_scalar(out=half_w[:], in0=weight_bf[:], scalar1=0.5, scalar2=None, op0=ALU.mult)
+        nc.vector.tensor_copy(out=gamma[:], in_=gamma_bf[:])
+        nc.vector.tensor_tensor(out=gamma_bias[:], in0=gamma_bf[:], in1=bias_bf[:], op=ALU.mult)
+        sum_positions(0)
+        add_streams(0)
+        move_means(0)
+        for t in range(PACK):
+            transpose_slot(0, t)
+
+        for u in range(PASSES):
+            weights_now = range(4 * u, 4 * u + 4) if u < 2 else ()
+            outputs_now = {3: range(6)}.get(u, ())
+            if u + 1 < PASSES:
+                sum_positions(u + 1)
+            for m in weights_now[:2]:
+                transpose_weights(m)
+            deviations(u)
+            if u + 1 < PASSES:
+                add_streams(u + 1)
+                move_means(u + 1)
+            for m in weights_now[:2]:
+                copy_weights(m)
+            factors(u)
+            for m in weights_now[2:]:
+                transpose_weights(m)
+            for t in range(PACK):
+                scale_slot(u, t)
+                if u + 1 < PASSES:
+                    transpose_slot(u + 1, t)
+            for m in weights_now[2:]:
+                copy_weights(m)
+            for m in outputs_now:
+                multiply(0, m)
+            for m in weights_now[::2]:
+                quantise_weights(m // 2)
+            if u == 3:
+                for m in outputs_now:
+                    finish(0, m)
+            regroup(u)
+            if u == 2:
+                for m in range(ROW_TILES):
+                    residual(0, m)
+            if u < 3:
+                quantise_stream(u)
+
+        for m in range(ROW_TILES):
+            residual(1, m)
+        for m in (6, 7):
+            multiply(0, m)
+        quantise_stream(3)
+        for m in (6, 7):
+            finish(0, m)
+        for m in range(3):
+            multiply(1, m)
+        for m in range(ROW_TILES):
+            finish(1, m)
+            if m + 3 < ROW_TILES:
+                multiply(1, m + 3)

@@ -31,7 +31,7 @@ def tile_axialattentionblock_pb_kernel(tc, xx, xy, x, norm2_w, out_w, out_b, gam
         const = ctx.enter_context(tc.tile_pool(name="const", bufs=1))
         inputs = ctx.enter_context(tc.tile_pool(name="inputs", bufs=1))
         keep = ctx.enter_context(tc.tile_pool(name="keep", bufs=1))
-        sums = ctx.enter_context(tc.tile_pool(name="sums", bufs=2))
+        sums = ctx.enter_context(tc.tile_pool(name="sums", bufs=3))
         stage = ctx.enter_context(tc.tile_pool(name="stage", bufs=2))
         small = ctx.enter_context(tc.tile_pool(name="small", bufs=4))
         ps_heads = ctx.enter_context(tc.psum_pool(name="ps_heads", bufs=4))
@@ -89,16 +89,17 @@ def tile_axialattentionblock_pb_kernel(tc, xx, xy, x, norm2_w, out_w, out_b, gam
         make_identity(nc, ident[:])
 
         load_pair(0, True)
-        for k in (1, 2, 3):
-            load_pair(k, False)
+        load_pair(1, False)
+        load_pair(2, False)
+        load_pair(3, False)
         load_weights(0)
         load_weights(1)
         load_pair(4, False)
         load_pair(5, False)
         load_weights(2)
         load_weights(3)
-        load_pair(6, False)
         load_residual(0)
+        load_pair(6, False)
         load_pair(7, False)
         load_residual(1)
 
@@ -111,6 +112,8 @@ def tile_axialattentionblock_pb_kernel(tc, xx, xy, x, norm2_w, out_w, out_b, gam
         gamma_bias = const.tile([P, ROW_TILES], F32, name="gamma_bias")
 
         head_mean = {}
+        spread_mean = {}
+        moved_mean = {}
         minus_mean = {}
         summed = {}
         slot_ps = {}
@@ -132,23 +135,29 @@ def tile_axialattentionblock_pb_kernel(tc, xx, xy, x, norm2_w, out_w, out_b, gam
                                      start=(i == 0), stop=(i == len(blocks) - 1))
             head_mean[u] = t
 
-        def add_streams(u):
-            s = sums.tile([P, CHUNKS, PACK, HEADS, QUADS], F32, name="summed")
-            for n in range(HEADS):
-                k, j = 2 * u + n // 2, n % 2
-                a, b = [src[k][:, j, :].rearrange("p (r q t) -> p r t q", r=CHUNKS, t=PACK) for src in (xx_sb, xy_sb)]
-                nc.vector.tensor_tensor(out=s[:, :, :, n, :], in0=a, in1=b, op=ALU.add)
-            summed[u] = s
+        def add_head(u, n):
+            if n == 0:
+                fresh = sums.tile([P, CHUNKS, PACK, HEADS, QUADS], F32, name="summed")
+                summed[u] = fresh
+            k, j = 2 * u + n // 2, n % 2
+            a, b = [src[k][:, j, :].rearrange("p (r q t) -> p r t q", r=CHUNKS, t=PACK) for src in (xx_sb, xy_sb)]
+            nc.vector.tensor_tensor(out=summed[u][:, :, :, n, :], in0=a, in1=b, op=ALU.add)
 
-        def move_means(u):
+        def spread_means(u):
             spread = small.tile([P, HEADS, QUADS], F32, name="spread")
+            spread_mean[u] = spread
             nc.vector.tensor_tensor(
                 out=spread[:], in0=same_quad[:].unsqueeze(1).to_broadcast([P, HEADS, QUADS]),
                 in1=head_mean[u][:, :, 0:1].to_broadcast([P, HEADS, QUADS]), op=ALU.mult)
+
+        def gather_means(u):
             moved = ps_products.tile([P, PACK], F32, name="moved", tag="products")
-            nc.tensor.matmul(moved[:], lhsT=spread[:].rearrange("p n q -> p (n q)"), rhs=same_slot[:], start=True, stop=True)
+            moved_mean[u] = moved
+            nc.tensor.matmul(moved[:], lhsT=spread_mean[u][:].rearrange("p n q -> p (n q)"), rhs=same_slot[:], start=True, stop=True)
+
+        def fetch_means(u):
             t = small.tile([P, PACK], F32, name="minus_mean")
-            nc.vector.tensor_copy(out=t[:], in_=moved[:])
+            nc.vector.tensor_copy(out=t[:], in_=moved_mean[u][:])
             minus_mean[u] = t
 
         def transpose_slot(u, t):
@@ -221,9 +230,9 @@ def tile_axialattentionblock_pb_kernel(tc, xx, xy, x, norm2_w, out_w, out_b, gam
             dst = w_grouped[m // 2][:, i].bitcast(F32)
             src = w_ps[m][:].rearrange("p g h o -> p g o h")
             if i == 0:
-                nc.scalar.copy(out=dst, in_=src)
-            else:
                 nc.vector.tensor_copy(out=dst, in_=src)
+            else:
+                nc.scalar.copy(out=dst, in_=src)
 
         def quantise_weights(i):
             codes = keep.tile([P, 4, P], U32, name="w_codes%d" % i, align_bytes=64)
@@ -278,47 +287,64 @@ def tile_axialattentionblock_pb_kernel(tc, xx, xy, x, norm2_w, out_w, out_b, gam
         nc.vector.tensor_copy(out=gamma[:], in_=gamma_bf[:])
         nc.vector.tensor_tensor(out=gamma_bias[:], in0=gamma_bf[:], in1=bias_bf[:], op=ALU.mult)
         sum_positions(0)
-        add_streams(0)
-        move_means(0)
+        for n in range(HEADS):
+            add_head(0, n)
+        spread_means(0)
+        gather_means(0)
         for t in range(PACK):
             transpose_slot(0, t)
+        add_head(1, 0)
+        fetch_means(0)
+        sum_positions(1)
+        for n in (1, 2, 3):
+            add_head(1, n)
+        spread_means(1)
+        gather_means(1)
 
         for u in range(PASSES):
-            weights_now = range(4 * u, 4 * u + 4) if u < 2 else ()
-            outputs_now = {3: range(6)}.get(u, ())
-            if u + 1 < PASSES:
-                sum_positions(u + 1)
-            for m in weights_now[:2]:
+            weights_now = (2 * u, 2 * u + 1)
+            for m in weights_now:
                 transpose_weights(m)
+            if u + 2 < PASSES:
+                sum_positions(u + 2)
             deviations(u)
+            if u >= 1:
+                regroup(u - 1)
             if u + 1 < PASSES:
-                add_streams(u + 1)
-                move_means(u + 1)
-            for m in weights_now[:2]:
-                copy_weights(m)
+                fetch_means(u + 1)
+            if u >= 1:
+                quantise_stream(u - 1)
+            copy_weights(2 * u)
             factors(u)
-            for m in weights_now[2:]:
-                transpose_weights(m)
+            copy_weights(2 * u + 1)
+            if u + 2 < PASSES:
+                spread_means(u + 2)
+                for n in range(HEADS):
+                    add_head(u + 2, n)
+            if u == 2:
+                for m in range(ROW_TILES):
+                    residual(0, m)
+                for m in (0, 1):
+                    multiply(0, m)
+                for m in (0, 1):
+                    finish(0, m)
+            if u == 3:
+                for m in (2, 3):
+                    multiply(0, m)
+                for m in (2, 3):
+                    finish(0, m)
             for t in range(PACK):
                 scale_slot(u, t)
                 if u + 1 < PASSES:
                     transpose_slot(u + 1, t)
-            for m in weights_now[2:]:
-                copy_weights(m)
-            for m in outputs_now:
-                multiply(0, m)
-            for m in weights_now[::2]:
-                quantise_weights(m // 2)
-            if u == 3:
-                for m in outputs_now:
-                    finish(0, m)
-            regroup(u)
-            if u == 2:
-                for m in range(ROW_TILES):
-                    residual(0, m)
-            if u < 3:
-                quantise_stream(u)
-
+            if u + 2 < PASSES:
+                gather_means(u + 2)
+            quantise_weights(u)
+        for m in (4, 5):
+            multiply(0, m)
+        for m in (4, 5):
+            finish(0, m)
+        regroup(3)
         for m in range(ROW_TILES):
             residual(1, m)
         for m in (6, 7):

@@ -22,6 +22,7 @@ QUADS = 32
 PACK = 4
 PASSES = 4
 ROW_TILES = 8
+ADDED_ON_TENSOR = (3,)
 MEAN_COLUMNS = 2
 
 
@@ -47,8 +48,9 @@ def tile_axialattentionblock_pb_kernel(tc, xx, xy, x, norm2_w, out_w, out_b, gam
             nc.scalar.dma_start(out=gamma_bf[:], in_=gamma_att.rearrange("(p m) -> p m", m=ROW_TILES))
             nc.scalar.dma_start(out=bias_bf[:], in_=out_b.rearrange("(p m) -> p m", m=ROW_TILES))
 
-        xx_sb = []
-        xy_sb = []
+        streams = {}
+        xx_sb = {}
+        xy_sb = {}
         w_sb = []
         x_sb = []
 
@@ -57,7 +59,7 @@ def tile_axialattentionblock_pb_kernel(tc, xx, xy, x, norm2_w, out_w, out_b, gam
             tiles = []
             for name, tiles_of in (("xx", xx_sb), ("xy", xy_sb)):
                 t = inputs.tile([P, 2, POSITIONS], BF16, name="%s_%d" % (name, k))
-                tiles_of.append(t)
+                tiles_of[k] = t
                 tiles.append(t)
             if by_head:
                 for j in range(2):
@@ -68,6 +70,16 @@ def tile_axialattentionblock_pb_kernel(tc, xx, xy, x, norm2_w, out_w, out_b, gam
                 for src, t in zip((xx, xy), tiles):
                     nc.sync.dma_start(
                         out=t[:], in_=src[b, n0:n0 + 2].rearrange("n h (q r) c -> (h q) n (r c)", r=CHUNKS))
+
+        def load_pass(u):
+            b, n0 = u // 2, 4 * (u % 2)
+            for name, src in (("xx", xx), ("xy", xy)):
+                t = inputs.tile([P, CHUNKS, HEADS, P], BF16, name="%s_pass%d" % (name, u))
+                streams[(name, u)] = t
+            for n in range(HEADS):
+                for name, src in (("xx", xx), ("xy", xy)):
+                    nc.sync.dma_start(out=streams[(name, u)][:, :, n, :],
+                                      in_=src[b, n0 + n].rearrange("h (q r) c -> (h q) r c", r=CHUNKS))
 
         def load_weights(i):
             t = inputs.tile([P, 2, 1024], BF16, name="w_sb%d" % i)
@@ -87,20 +99,21 @@ def tile_axialattentionblock_pb_kernel(tc, xx, xy, x, norm2_w, out_w, out_b, gam
         nc.vector.memset(minus_mean_weight[:], -1.0 / POSITIONS)
         ident = const.tile([P, P], F32, name="ident")
         make_identity(nc, ident[:])
+        ident_bf = const.tile([P, P], BF16, name="ident_bf")
+        nc.vector.tensor_copy(out=ident_bf[:], in_=ident[:])
 
         load_pair(0, True)
         load_pair(1, False)
+        load_weights(0)
         load_pair(2, False)
         load_pair(3, False)
-        load_weights(0)
         load_weights(1)
         load_pair(4, False)
         load_pair(5, False)
         load_weights(2)
-        load_weights(3)
+        load_pass(3)
         load_residual(0)
-        load_pair(6, False)
-        load_pair(7, False)
+        load_weights(3)
         load_residual(1)
 
         same_quad = const.tile([P, QUADS], F32, name="same_quad")
@@ -125,7 +138,19 @@ def tile_axialattentionblock_pb_kernel(tc, xx, xy, x, norm2_w, out_w, out_b, gam
         g_codes = {}
         g_scales = {}
 
+        def slot_columns(name, u, r, t):
+            return streams[(name, u)][:, r].rearrange("i n c -> i (n c)")[:, t::PACK]
+
         def sum_positions(u):
+            if u in ADDED_ON_TENSOR:
+                t = ps_products.tile([P, PACK, MEAN_COLUMNS], F32, name="mean_ps", tag="products")
+                for slot in range(PACK):
+                    blocks = [slot_columns(name, u, r, slot) for name in ("xx", "xy") for r in range(CHUNKS)]
+                    for i, block in enumerate(blocks):
+                        nc.tensor.matmul(t[:, slot, :], lhsT=block, rhs=minus_mean_weight[:],
+                                         start=(i == 0), stop=(i == len(blocks) - 1))
+                moved_mean[u] = t
+                return
             t = ps_products.tile([P, HEADS, MEAN_COLUMNS], F32, name="mean_ps", tag="products")
             for n in range(HEADS):
                 k, j = 2 * u + n // 2, n % 2
@@ -151,40 +176,47 @@ def tile_axialattentionblock_pb_kernel(tc, xx, xy, x, norm2_w, out_w, out_b, gam
                 in1=head_mean[u][:, :, 0:1].to_broadcast([P, HEADS, QUADS]), op=ALU.mult)
 
         def gather_means(u):
-            moved = ps_products.tile([P, PACK], F32, name="moved", tag="products")
+            moved = ps_products.tile([P, PACK, 1], F32, name="moved", tag="products")
             moved_mean[u] = moved
-            nc.tensor.matmul(moved[:], lhsT=spread_mean[u][:].rearrange("p n q -> p (n q)"), rhs=same_slot[:], start=True, stop=True)
+            nc.tensor.matmul(moved[:, :, 0], lhsT=spread_mean[u][:].rearrange("p n q -> p (n q)"), rhs=same_slot[:], start=True, stop=True)
 
         def fetch_means(u):
             t = small.tile([P, PACK], F32, name="minus_mean")
-            nc.vector.tensor_copy(out=t[:], in_=moved_mean[u][:])
+            nc.vector.tensor_copy(out=t[:], in_=moved_mean[u][:, :, 0])
             minus_mean[u] = t
 
         def transpose_slot(u, t):
             bank = ps_heads.tile([P, POSITIONS], F32, name="slot_ps", tag="heads")
             for r in range(CHUNKS):
+                cols = slice(P * r, P * r + P)
+                if u in ADDED_ON_TENSOR:
+                    nc.tensor.matmul(bank[:, cols], lhsT=slot_columns("xx", u, r, t), rhs=ident_bf[:], start=True, stop=False)
+                    nc.tensor.matmul(bank[:, cols], lhsT=slot_columns("xy", u, r, t), rhs=ident_bf[:], start=False, stop=True)
+                    continue
                 nc.tensor.transpose(bank[:, P * r:P * r + P], summed[u][:, r, t, :, :].rearrange("p n q -> p (n q)"), ident[:])
             slot_ps[(u, t)] = bank
 
-        def deviations(u):
-            sq = small.tile([P, PACK], F32, name="square_sum")
-            for t in range(PACK):
-                unused = small.tile([P, POSITIONS], BF16, name="unused")
-                nc.scalar.activation(out=unused[:], in_=slot_ps[(u, t)][:], func=ACT.Square,
-                                     bias=minus_mean[u][:, t:t + 1], scale=1.0, accum_out=sq[:, t:t + 1])
-            square_sum[u] = sq
-            d = small.tile([P, PACK], F32, name="deviation")
-            nc.scalar.activation(out=d[:], in_=sq[:], func=ACT.Sqrt, scale=1.0 / (4.0 * (POSITIONS - 1)))
-            deviation[u] = d
+        def square_slot(u, t):
+            if t % 2 == 0:
+                fresh = small.tile([P, 2], F32, name="square_sum")
+                square_sum[(u, t // 2)] = fresh
+            unused = small.tile([P, POSITIONS], BF16, name="unused")
+            nc.scalar.activation(out=unused[:], in_=slot_ps[(u, t)][:], func=ACT.Square, bias=minus_mean[u][:, t:t + 1],
+                                 scale=1.0, accum_out=square_sum[(u, t // 2)][:, t % 2:t % 2 + 1])
 
-        def factors(u):
-            denominator = small.tile([P, PACK], F32, name="denominator")
-            nc.vector.tensor_scalar(out=denominator[:], in0=deviation[u][:], scalar1=1e-8, scalar2=None, op0=ALU.add)
-            inverse = small.tile([P, PACK], F32, name="inverse")
+        def deviations(u, i):
+            d = small.tile([P, 2], F32, name="deviation")
+            nc.scalar.activation(out=d[:], in_=square_sum[(u, i)][:], func=ACT.Sqrt, scale=1.0 / (4.0 * (POSITIONS - 1)))
+            deviation[(u, i)] = d
+
+        def factors(u, i):
+            denominator = small.tile([P, 2], F32, name="denominator")
+            nc.vector.tensor_scalar(out=denominator[:], in0=deviation[(u, i)][:], scalar1=1e-8, scalar2=None, op0=ALU.add)
+            inverse = small.tile([P, 2], F32, name="inverse")
             nc.vector.reciprocal(out=inverse[:], in_=denominator[:])
-            f = small.tile([P, PACK], F32, name="factor")
-            nc.vector.tensor_tensor(out=f[:], in0=inverse[:], in1=half_w[:, u % 2, :], op=ALU.mult)
-            factor[u] = f
+            f = small.tile([P, 2], F32, name="factor")
+            nc.vector.tensor_tensor(out=f[:], in0=inverse[:], in1=half_w[:, u % 2, 2 * i:2 * i + 2], op=ALU.mult)
+            factor[(u, i)] = f
 
         def scale_slot(u, t):
             if t == 0:
@@ -193,7 +225,7 @@ def tile_axialattentionblock_pb_kernel(tc, xx, xy, x, norm2_w, out_w, out_b, gam
             nc.scalar.activation(
                 out=scaled[u][:, t, :].rearrange("c (p r) -> c p r", r=CHUNKS),
                 in_=slot_ps[(u, t)][:].rearrange("c (r p) -> c p r", r=CHUNKS),
-                func=ACT.Copy, scale=factor[u][:, t:t + 1])
+                func=ACT.Copy, scale=factor[(u, t // 2)][:, t % 2:t % 2 + 1])
 
         def regroup(u):
             t = stage.tile([P, POSITIONS, PACK], BF16, name="grouped", align_bytes=64)
@@ -224,7 +256,7 @@ def tile_axialattentionblock_pb_kernel(tc, xx, xy, x, norm2_w, out_w, out_b, gam
 
         def copy_weights(m):
             i = m % 2
-            if i == 0:
+            if m // 2 not in w_grouped:
                 fresh = stage.tile([P, 2, 2, P, PACK], BF16, name="w_grouped", align_bytes=64)
                 w_grouped[m // 2] = fresh
             dst = w_grouped[m // 2][:, i].bitcast(F32)
@@ -251,7 +283,7 @@ def tile_axialattentionblock_pb_kernel(tc, xx, xy, x, norm2_w, out_w, out_b, gam
                 fresh = keep.tile([P, 2, POSITIONS], F32, name="result%d%d" % (b, m // 2))
                 result[(b, m // 2)] = fresh
             dst = result[(b, m // 2)][:, m % 2, :]
-            if b == 0:
+            if b == 0 and m < 4:
                 nc.vector.tensor_scalar(out=dst, in0=x_sb[b][:, m, :], scalar1=1.0, scalar2=gamma_bias[:, m:m + 1],
                                         op0=ALU.mult, op1=ALU.add)
             else:
@@ -259,8 +291,10 @@ def tile_axialattentionblock_pb_kernel(tc, xx, xy, x, norm2_w, out_w, out_b, gam
                                      bias=gamma_bias[:, m:m + 1], scale=1.0)
 
         def multiply(b, m):
-            if b == 0:
+            if b == 0 and m < 6:
                 t = ps_products.tile([P, POSITIONS], F32, name="product", tag="products")
+            elif b == 0:
+                t = ps_weights.tile([P, POSITIONS], F32, name="product", tag="w_ps")
             else:
                 t = ps_heads.tile([P, POSITIONS], F32, name="product", tag="heads")
             for g in range(2):
@@ -293,64 +327,61 @@ def tile_axialattentionblock_pb_kernel(tc, xx, xy, x, norm2_w, out_w, out_b, gam
         gather_means(0)
         for t in range(PACK):
             transpose_slot(0, t)
-        add_head(1, 0)
         fetch_means(0)
-        sum_positions(1)
-        for n in (1, 2, 3):
+        for n in range(HEADS):
             add_head(1, n)
-        spread_means(1)
-        gather_means(1)
 
         for u in range(PASSES):
-            weights_now = (2 * u, 2 * u + 1)
-            for m in weights_now:
-                transpose_weights(m)
-            if u + 2 < PASSES:
-                sum_positions(u + 2)
-            deviations(u)
+            transpose_weights(2 * u)
+            transpose_weights(2 * u + 1)
+            if u + 1 < PASSES:
+                sum_positions(u + 1)
+            square_slot(u, 0)
+            square_slot(u, 1)
+            square_slot(u, 2)
+            deviations(u, 0)
+            square_slot(u, 3)
             if u >= 1:
                 regroup(u - 1)
+                quantise_stream(u - 1)
+            factors(u, 0)
+            copy_weights(2 * u + 1)
+            deviations(u, 1)
+            copy_weights(2 * u)
+            factors(u, 1)
+            if u + 1 < PASSES:
+                if u + 1 not in ADDED_ON_TENSOR:
+                    spread_means(u + 1)
+                    gather_means(u + 1)
+            adding = u + 2 < PASSES and u + 2 not in ADDED_ON_TENSOR
+            if adding:
+                add_head(u + 2, 0)
+                add_head(u + 2, 1)
+            quantise_weights(u)
             if u + 1 < PASSES:
                 fetch_means(u + 1)
-            if u >= 1:
-                quantise_stream(u - 1)
-            copy_weights(2 * u)
-            factors(u)
-            copy_weights(2 * u + 1)
-            if u + 2 < PASSES:
-                spread_means(u + 2)
-                for n in range(HEADS):
-                    add_head(u + 2, n)
-            if u == 2:
-                for m in range(ROW_TILES):
+            if adding:
+                add_head(u + 2, 2)
+                add_head(u + 2, 3)
+            if u >= 2:
+                for m in (2 * u - 4, 2 * u - 3):
                     residual(0, m)
-                for m in (0, 1):
                     multiply(0, m)
-                for m in (0, 1):
-                    finish(0, m)
-            if u == 3:
-                for m in (2, 3):
-                    multiply(0, m)
-                for m in (2, 3):
+            if u >= 2:
+                for m in (2 * u - 4, 2 * u - 3):
                     finish(0, m)
             for t in range(PACK):
                 scale_slot(u, t)
                 if u + 1 < PASSES:
                     transpose_slot(u + 1, t)
-            if u + 2 < PASSES:
-                gather_means(u + 2)
-            quantise_weights(u)
-        for m in (4, 5):
-            multiply(0, m)
-        for m in (4, 5):
-            finish(0, m)
         regroup(3)
+        for m in (4, 5, 6, 7):
+            residual(0, m)
+            multiply(0, m)
         for m in range(ROW_TILES):
             residual(1, m)
-        for m in (6, 7):
-            multiply(0, m)
         quantise_stream(3)
-        for m in (6, 7):
+        for m in (4, 5, 6, 7):
             finish(0, m)
         for m in range(3):
             multiply(1, m)

@@ -22,7 +22,11 @@ QUADS = 32
 PACK = 4
 PASSES = 4
 ROW_TILES = 8
-ADDED_ON_TENSOR = (3,)
+TENSOR_CHUNKS = {2: 2, 3: 4}
+ADDED_ON_TENSOR = (2, 3)
+W_V = (0, 2, 4, 6)
+RES_V = ((0, 0), (0, 1), (0, 2), (0, 3))
+RES_G = ()
 MEAN_COLUMNS = 2
 
 
@@ -108,8 +112,7 @@ def tile_axialattentionblock_pb_kernel(tc, xx, xy, x, norm2_w, out_w, out_b, gam
         load_pair(2, False)
         load_pair(3, False)
         load_weights(1)
-        load_pair(4, False)
-        load_pair(5, False)
+        load_pass(2)
         load_weights(2)
         load_pass(3)
         load_residual(0)
@@ -168,6 +171,13 @@ def tile_axialattentionblock_pb_kernel(tc, xx, xy, x, norm2_w, out_w, out_b, gam
             a, b = [src[k][:, j, :].rearrange("p (r q t) -> p r t q", r=CHUNKS, t=PACK) for src in (xx_sb, xy_sb)]
             nc.vector.tensor_tensor(out=summed[u][:, :, :, n, :], in0=a, in1=b, op=ALU.add)
 
+        def add_chunk(u, r):
+            if u not in summed:
+                fresh = sums.tile([P, CHUNKS, PACK, HEADS, QUADS], F32, name="summed")
+                summed[u] = fresh
+            a, b = [streams[(name, u)][:, r].rearrange("p n (q t) -> p t n q", t=PACK) for name in ("xx", "xy")]
+            nc.vector.tensor_tensor(out=summed[u][:, r], in0=a, in1=b, op=ALU.add)
+
         def spread_means(u):
             spread = small.tile([P, HEADS, QUADS], F32, name="spread")
             spread_mean[u] = spread
@@ -189,7 +199,7 @@ def tile_axialattentionblock_pb_kernel(tc, xx, xy, x, norm2_w, out_w, out_b, gam
             bank = ps_heads.tile([P, POSITIONS], F32, name="slot_ps", tag="heads")
             for r in range(CHUNKS):
                 cols = slice(P * r, P * r + P)
-                if u in ADDED_ON_TENSOR:
+                if r < TENSOR_CHUNKS.get(u, 0):
                     nc.tensor.matmul(bank[:, cols], lhsT=slot_columns("xx", u, r, t), rhs=ident_bf[:], start=True, stop=False)
                     nc.tensor.matmul(bank[:, cols], lhsT=slot_columns("xy", u, r, t), rhs=ident_bf[:], start=False, stop=True)
                     continue
@@ -229,8 +239,14 @@ def tile_axialattentionblock_pb_kernel(tc, xx, xy, x, norm2_w, out_w, out_b, gam
 
         def regroup(u):
             t = stage.tile([P, POSITIONS, PACK], BF16, name="grouped", align_bytes=64)
-            nc.vector.tensor_copy(out=t[:].rearrange("p (c i) t -> p c t i", i=4),
-                                  in_=scaled[u][:].rearrange("p t (c i) -> p c t i", i=4))
+            dst = t[:].rearrange("p (c i) t -> p c t i", i=4)
+            src = scaled[u][:].rearrange("p t (c i) -> p c t i", i=4)
+            if u == 3 and True:
+                k = 84
+                nc.vector.tensor_copy(out=dst[:, :k], in_=src[:, :k])
+                nc.scalar.copy(out=dst[:, k:], in_=src[:, k:])
+            else:
+                nc.vector.tensor_copy(out=dst, in_=src)
             grouped[u] = t
 
         def quantise_stream(u):
@@ -261,7 +277,7 @@ def tile_axialattentionblock_pb_kernel(tc, xx, xy, x, norm2_w, out_w, out_b, gam
                 w_grouped[m // 2] = fresh
             dst = w_grouped[m // 2][:, i].bitcast(F32)
             src = w_ps[m][:].rearrange("p g h o -> p g o h")
-            if i == 0:
+            if m in W_V:
                 nc.vector.tensor_copy(out=dst, in_=src)
             else:
                 nc.scalar.copy(out=dst, in_=src)
@@ -283,12 +299,22 @@ def tile_axialattentionblock_pb_kernel(tc, xx, xy, x, norm2_w, out_w, out_b, gam
                 fresh = keep.tile([P, 2, POSITIONS], F32, name="result%d%d" % (b, m // 2))
                 result[(b, m // 2)] = fresh
             dst = result[(b, m // 2)][:, m % 2, :]
-            if b == 0 and m < 4:
+            if (b, m) in RES_V:
                 nc.vector.tensor_scalar(out=dst, in0=x_sb[b][:, m, :], scalar1=1.0, scalar2=gamma_bias[:, m:m + 1],
+                                        op0=ALU.mult, op1=ALU.add)
+            elif (b, m) in RES_G:
+                nc.gpsimd.tensor_scalar(out=dst, in0=x_sb[b][:, m, :], scalar1=1.0, scalar2=(gamma_bias if b == 0 else late_bias[0])[:, m:m + 1],
                                         op0=ALU.mult, op1=ALU.add)
             else:
                 nc.scalar.activation(out=dst, in_=x_sb[b][:, m, :], func=ACT.Identity,
                                      bias=gamma_bias[:, m:m + 1], scale=1.0)
+
+        late_bias = []
+
+        def open_late_bias():
+            t = const.tile([P, ROW_TILES], F32, name="late_bias")
+            nc.vector.tensor_copy(out=t[:], in_=gamma_bias[:])
+            late_bias.append(t)
 
         def multiply(b, m):
             if b == 0 and m < 6:
@@ -312,7 +338,7 @@ def tile_axialattentionblock_pb_kernel(tc, xx, xy, x, norm2_w, out_w, out_b, gam
             nc.vector.scalar_tensor_tensor(out=t[:, m % 2, :], in0=product[(b, m)][:], scalar=gamma[:, m:m + 1],
                                            in1=t[:, m % 2, :], op0=ALU.mult, op1=ALU.add)
             view = out[b].rearrange("(p m) h w -> p m (h w)", m=ROW_TILES)
-            if b == 1:
+            if b == 1 or m >= 4:
                 nc.sync.dma_start(out=view[:, m, :], in_=t[:, m % 2, :])
             elif m % 2 == 1:
                 nc.sync.dma_start(out=view[:, m - 1:m + 1, :], in_=t[:])
@@ -332,8 +358,9 @@ def tile_axialattentionblock_pb_kernel(tc, xx, xy, x, norm2_w, out_w, out_b, gam
             add_head(1, n)
 
         for u in range(PASSES):
-            transpose_weights(2 * u)
-            transpose_weights(2 * u + 1)
+            pair = (2 * u, 2 * u + 1)
+            for m in pair:
+                transpose_weights(m)
             if u + 1 < PASSES:
                 sum_positions(u + 1)
             square_slot(u, 0)
@@ -345,43 +372,39 @@ def tile_axialattentionblock_pb_kernel(tc, xx, xy, x, norm2_w, out_w, out_b, gam
                 regroup(u - 1)
                 quantise_stream(u - 1)
             factors(u, 0)
-            copy_weights(2 * u + 1)
             deviations(u, 1)
+            copy_weights(2 * u + 1)
             copy_weights(2 * u)
             factors(u, 1)
-            if u + 1 < PASSES:
-                if u + 1 not in ADDED_ON_TENSOR:
-                    spread_means(u + 1)
-                    gather_means(u + 1)
-            adding = u + 2 < PASSES and u + 2 not in ADDED_ON_TENSOR
+            if u + 1 < PASSES and u + 1 not in ADDED_ON_TENSOR:
+                spread_means(u + 1)
+                gather_means(u + 1)
+            adding = u == 1
             if adding:
-                add_head(u + 2, 0)
-                add_head(u + 2, 1)
+                add_chunk(u + 1, 2)
+                add_chunk(u + 1, 3)
             quantise_weights(u)
             if u + 1 < PASSES:
                 fetch_means(u + 1)
-            if adding:
-                add_head(u + 2, 2)
-                add_head(u + 2, 3)
             if u >= 2:
-                for m in (2 * u - 4, 2 * u - 3):
+                for m in {2: [0,1], 3: [2,3]}[u]:
                     residual(0, m)
                     multiply(0, m)
-            if u >= 2:
-                for m in (2 * u - 4, 2 * u - 3):
+                for m in {2: [0,1], 3: [2,3]}[u]:
                     finish(0, m)
             for t in range(PACK):
                 scale_slot(u, t)
                 if u + 1 < PASSES:
                     transpose_slot(u + 1, t)
         regroup(3)
-        for m in (4, 5, 6, 7):
+        for m in [4,5,6,7]:
             residual(0, m)
             multiply(0, m)
+        quantise_stream(3)
+        open_late_bias()
         for m in range(ROW_TILES):
             residual(1, m)
-        quantise_stream(3)
-        for m in (4, 5, 6, 7):
+        for m in [4,5,6,7]:
             finish(0, m)
         for m in range(3):
             multiply(1, m)

@@ -22,8 +22,7 @@ QUADS = 32
 PACK = 4
 PASSES = 4
 ROW_TILES = 8
-TENSOR_CHUNKS = {2: 2, 3: 4}
-ADDED_ON_TENSOR = (2, 3)
+ADDED_ON_TENSOR = (3,)
 W_V = (0, 2, 4, 6)
 RES_V = ((0, 0), (0, 1), (0, 2), (0, 3))
 RES_G = ()
@@ -107,12 +106,13 @@ def tile_axialattentionblock_pb_kernel(tc, xx, xy, x, norm2_w, out_w, out_b, gam
         nc.vector.tensor_copy(out=ident_bf[:], in_=ident[:])
 
         load_pair(0, True)
-        load_pair(1, False)
+        load_pair(1, True)
         load_weights(0)
         load_pair(2, False)
         load_pair(3, False)
         load_weights(1)
-        load_pass(2)
+        load_pair(4, False)
+        load_pair(5, False)
         load_weights(2)
         load_pass(3)
         load_residual(0)
@@ -171,13 +171,6 @@ def tile_axialattentionblock_pb_kernel(tc, xx, xy, x, norm2_w, out_w, out_b, gam
             a, b = [src[k][:, j, :].rearrange("p (r q t) -> p r t q", r=CHUNKS, t=PACK) for src in (xx_sb, xy_sb)]
             nc.vector.tensor_tensor(out=summed[u][:, :, :, n, :], in0=a, in1=b, op=ALU.add)
 
-        def add_chunk(u, r):
-            if u not in summed:
-                fresh = sums.tile([P, CHUNKS, PACK, HEADS, QUADS], F32, name="summed")
-                summed[u] = fresh
-            a, b = [streams[(name, u)][:, r].rearrange("p n (q t) -> p t n q", t=PACK) for name in ("xx", "xy")]
-            nc.vector.tensor_tensor(out=summed[u][:, r], in0=a, in1=b, op=ALU.add)
-
         def spread_means(u):
             spread = small.tile([P, HEADS, QUADS], F32, name="spread")
             spread_mean[u] = spread
@@ -199,7 +192,7 @@ def tile_axialattentionblock_pb_kernel(tc, xx, xy, x, norm2_w, out_w, out_b, gam
             bank = ps_heads.tile([P, POSITIONS], F32, name="slot_ps", tag="heads")
             for r in range(CHUNKS):
                 cols = slice(P * r, P * r + P)
-                if r < TENSOR_CHUNKS.get(u, 0):
+                if u in ADDED_ON_TENSOR:
                     nc.tensor.matmul(bank[:, cols], lhsT=slot_columns("xx", u, r, t), rhs=ident_bf[:], start=True, stop=False)
                     nc.tensor.matmul(bank[:, cols], lhsT=slot_columns("xy", u, r, t), rhs=ident_bf[:], start=False, stop=True)
                     continue
@@ -354,12 +347,11 @@ def tile_axialattentionblock_pb_kernel(tc, xx, xy, x, norm2_w, out_w, out_b, gam
         for t in range(PACK):
             transpose_slot(0, t)
         fetch_means(0)
-        for n in range(HEADS):
-            add_head(1, n)
+        add_head(1, 0)
+        add_head(1, 1)
 
         for u in range(PASSES):
-            pair = (2 * u, 2 * u + 1)
-            for m in pair:
+            for m in (2 * u, 2 * u + 1):
                 transpose_weights(m)
             if u + 1 < PASSES:
                 sum_positions(u + 1)
@@ -368,24 +360,38 @@ def tile_axialattentionblock_pb_kernel(tc, xx, xy, x, norm2_w, out_w, out_b, gam
             square_slot(u, 2)
             deviations(u, 0)
             square_slot(u, 3)
+            deviations(u, 1)
+            copy_weights(2 * u + 1)
             if u >= 1:
                 regroup(u - 1)
                 quantise_stream(u - 1)
             factors(u, 0)
-            deviations(u, 1)
-            copy_weights(2 * u + 1)
-            copy_weights(2 * u)
-            factors(u, 1)
-            if u + 1 < PASSES and u + 1 not in ADDED_ON_TENSOR:
-                spread_means(u + 1)
-                gather_means(u + 1)
-            adding = u == 1
-            if adding:
-                add_chunk(u + 1, 2)
-                add_chunk(u + 1, 3)
-            quantise_weights(u)
-            if u + 1 < PASSES:
-                fetch_means(u + 1)
+            if u == 0:
+                add_head(1, 2)
+                factors(0, 1)
+                add_head(1, 3)
+                spread_means(1)
+                gather_means(1)
+                copy_weights(0)
+                add_head(2, 0)
+                fetch_means(1)
+                quantise_weights(0)
+                add_head(2, 1)
+            elif u == 1:
+                factors(1, 1)
+                spread_means(2)
+                gather_means(2)
+                add_head(2, 2)
+                add_head(2, 3)
+                fetch_means(2)
+                copy_weights(2)
+                quantise_weights(1)
+            else:
+                copy_weights(2 * u)
+                if u == 2:
+                    fetch_means(3)
+                factors(u, 1)
+                quantise_weights(u)
             if u >= 2:
                 for m in {2: [0,1], 3: [2,3]}[u]:
                     residual(0, m)

@@ -24,7 +24,7 @@ PASSES = 4
 ROW_TILES = 8
 ADDED_ON_TENSOR = (3,)
 W_V = (0, 2, 4, 6)
-RES_V = ((0, 0), (0, 1), (0, 2), (0, 3))
+RES_V = ((0, 0), (0, 1), (0, 2), (0, 3), (0, 4), (0, 5))
 RES_G = ()
 MEAN_COLUMNS = 2
 
@@ -135,6 +135,8 @@ def tile_axialattentionblock_pb_kernel(tc, xx, xy, x, norm2_w, out_w, out_b, gam
         slot_ps = {}
         square_sum = {}
         deviation = {}
+        denominator = {}
+        inverse = {}
         factor = {}
         scaled = {}
         grouped = {}
@@ -212,13 +214,19 @@ def tile_axialattentionblock_pb_kernel(tc, xx, xy, x, norm2_w, out_w, out_b, gam
             nc.scalar.activation(out=d[:], in_=square_sum[(u, i)][:], func=ACT.Sqrt, scale=1.0 / (4.0 * (POSITIONS - 1)))
             deviation[(u, i)] = d
 
+        def factor_denominator(u, i):
+            d = small.tile([P, 2], F32, name="denominator")
+            nc.vector.tensor_scalar(out=d[:], in0=deviation[(u, i)][:], scalar1=1e-8, scalar2=None, op0=ALU.add)
+            denominator[(u, i)] = d
+
+        def factor_inverse(u, i):
+            d = small.tile([P, 2], F32, name="inverse")
+            nc.vector.reciprocal(out=d[:], in_=denominator[(u, i)][:])
+            inverse[(u, i)] = d
+
         def factors(u, i):
-            denominator = small.tile([P, 2], F32, name="denominator")
-            nc.vector.tensor_scalar(out=denominator[:], in0=deviation[(u, i)][:], scalar1=1e-8, scalar2=None, op0=ALU.add)
-            inverse = small.tile([P, 2], F32, name="inverse")
-            nc.vector.reciprocal(out=inverse[:], in_=denominator[:])
             f = small.tile([P, 2], F32, name="factor")
-            nc.vector.tensor_tensor(out=f[:], in0=inverse[:], in1=half_w[:, u % 2, 2 * i:2 * i + 2], op=ALU.mult)
+            nc.vector.tensor_tensor(out=f[:], in0=inverse[(u, i)][:], in1=half_w[:, u % 2, 2 * i:2 * i + 2], op=ALU.mult)
             factor[(u, i)] = f
 
         def scale_slot(u, t):
@@ -362,35 +370,42 @@ def tile_axialattentionblock_pb_kernel(tc, xx, xy, x, norm2_w, out_w, out_b, gam
             square_slot(u, 3)
             deviations(u, 1)
             copy_weights(2 * u + 1)
-            if u >= 1:
-                regroup(u - 1)
-                quantise_stream(u - 1)
-            factors(u, 0)
             if u == 0:
+                factor_denominator(0, 0)
                 add_head(1, 2)
-                factors(0, 1)
-                add_head(1, 3)
+                factor_inverse(0, 0)
+                factor_denominator(0, 1)
                 spread_means(1)
                 gather_means(1)
+                factors(0, 0)
+                factor_inverse(0, 1)
+                add_head(1, 3)
+                factors(0, 1)
                 copy_weights(0)
-                add_head(2, 0)
                 fetch_means(1)
+                add_head(2, 0)
                 quantise_weights(0)
                 add_head(2, 1)
-            elif u == 1:
-                factors(1, 1)
-                spread_means(2)
-                gather_means(2)
-                add_head(2, 2)
-                add_head(2, 3)
-                fetch_means(2)
-                copy_weights(2)
-                quantise_weights(1)
             else:
+                regroup(u - 1)
                 copy_weights(2 * u)
+                factor_denominator(u, 0)
+                quantise_stream(u - 1)
+                factor_inverse(u, 0)
+                factor_denominator(u, 1)
+                if u == 1:
+                    spread_means(2)
+                    gather_means(2)
                 if u == 2:
                     fetch_means(3)
+                factors(u, 0)
+                factor_inverse(u, 1)
+                if u == 1:
+                    add_head(2, 2)
                 factors(u, 1)
+                if u == 1:
+                    add_head(2, 3)
+                    fetch_means(2)
                 quantise_weights(u)
             if u >= 2:
                 for m in {2: [0,1], 3: [2,3]}[u]:
@@ -406,12 +421,14 @@ def tile_axialattentionblock_pb_kernel(tc, xx, xy, x, norm2_w, out_w, out_b, gam
         for m in [4,5,6,7]:
             residual(0, m)
             multiply(0, m)
+        finish(0, 4)
+        finish(0, 5)
         quantise_stream(3)
         open_late_bias()
+        finish(0, 6)
+        finish(0, 7)
         for m in range(ROW_TILES):
             residual(1, m)
-        for m in [4,5,6,7]:
-            finish(0, m)
         for m in range(3):
             multiply(1, m)
         for m in range(ROW_TILES):

@@ -46,10 +46,6 @@ def tile_axialattentionblock_pb_kernel(tc, xx, xy, x, norm2_w, out_w, out_b, gam
         weight_bf = const.tile([P, 2, PACK], BF16, name="weight_bf")
         gamma_bf = const.tile([P, ROW_TILES], BF16, name="gamma_bf")
         bias_bf = const.tile([P, ROW_TILES], BF16, name="bias_bf")
-        with nc.allow_non_contiguous_dma(reason="three vectors of 1,024 values, eight values to a partition"):
-            nc.scalar.dma_start(out=weight_bf[:], in_=norm2_w.rearrange("(g p t) -> p g t", g=2, t=PACK))
-            nc.scalar.dma_start(out=gamma_bf[:], in_=gamma_att.rearrange("(p m) -> p m", m=ROW_TILES))
-            nc.scalar.dma_start(out=bias_bf[:], in_=out_b.rearrange("(p m) -> p m", m=ROW_TILES))
 
         streams = {}
         xx_sb = {}
@@ -107,14 +103,18 @@ def tile_axialattentionblock_pb_kernel(tc, xx, xy, x, norm2_w, out_w, out_b, gam
 
         load_pair(0, True)
         load_pair(1, True)
+        with nc.allow_non_contiguous_dma(reason="three vectors of 1,024 values, eight values to a partition"):
+            nc.sync.dma_start(out=weight_bf[:], in_=norm2_w.rearrange("(g p t) -> p g t", g=2, t=PACK))
+            nc.sync.dma_start(out=gamma_bf[:], in_=gamma_att.rearrange("(p m) -> p m", m=ROW_TILES))
+            nc.sync.dma_start(out=bias_bf[:], in_=out_b.rearrange("(p m) -> p m", m=ROW_TILES))
         load_weights(0)
         load_pair(2, False)
         load_pair(3, False)
-        load_weights(1)
         load_pair(4, False)
         load_pair(5, False)
-        load_weights(2)
+        load_weights(1)
         load_pass(3)
+        load_weights(2)
         load_residual(0)
         load_weights(3)
         load_residual(1)
@@ -344,9 +344,6 @@ def tile_axialattentionblock_pb_kernel(tc, xx, xy, x, norm2_w, out_w, out_b, gam
             elif m % 2 == 1:
                 nc.sync.dma_start(out=view[:, m - 1:m + 1, :], in_=t[:])
 
-        nc.vector.tensor_scalar(out=half_w[:], in0=weight_bf[:], scalar1=0.5, scalar2=None, op0=ALU.mult)
-        nc.vector.tensor_copy(out=gamma[:], in_=gamma_bf[:])
-        nc.vector.tensor_tensor(out=gamma_bias[:], in0=gamma_bf[:], in1=bias_bf[:], op=ALU.mult)
         sum_positions(0)
         for n in range(HEADS):
             add_head(0, n)
@@ -355,14 +352,19 @@ def tile_axialattentionblock_pb_kernel(tc, xx, xy, x, norm2_w, out_w, out_b, gam
         for t in range(PACK):
             transpose_slot(0, t)
         fetch_means(0)
+        nc.vector.tensor_scalar(out=half_w[:], in0=weight_bf[:], scalar1=0.5, scalar2=None, op0=ALU.mult)
+        nc.vector.tensor_copy(out=gamma[:], in_=gamma_bf[:])
+        nc.vector.tensor_tensor(out=gamma_bias[:], in0=gamma_bf[:], in1=bias_bf[:], op=ALU.mult)
         add_head(1, 0)
         add_head(1, 1)
 
         for u in range(PASSES):
-            for m in (2 * u, 2 * u + 1):
-                transpose_weights(m)
-            if u + 1 < PASSES:
+            if u != 0 and u + 1 < PASSES:
                 sum_positions(u + 1)
+            transpose_weights(2 * u)
+            transpose_weights(2 * u + 1)
+            if u == 0:
+                sum_positions(1)
             square_slot(u, 0)
             square_slot(u, 1)
             square_slot(u, 2)
@@ -372,63 +374,87 @@ def tile_axialattentionblock_pb_kernel(tc, xx, xy, x, norm2_w, out_w, out_b, gam
             copy_weights(2 * u + 1)
             if u == 0:
                 factor_denominator(0, 0)
-                add_head(1, 2)
+                copy_weights(0)
                 factor_inverse(0, 0)
                 factor_denominator(0, 1)
                 spread_means(1)
                 gather_means(1)
                 factors(0, 0)
                 factor_inverse(0, 1)
-                add_head(1, 3)
+                add_head(1, 2)
                 factors(0, 1)
-                copy_weights(0)
+                add_head(1, 3)
                 fetch_means(1)
-                add_head(2, 0)
                 quantise_weights(0)
+                add_head(2, 0)
                 add_head(2, 1)
-            else:
-                regroup(u - 1)
-                copy_weights(2 * u)
-                factor_denominator(u, 0)
-                quantise_stream(u - 1)
-                factor_inverse(u, 0)
-                factor_denominator(u, 1)
-                if u == 1:
-                    spread_means(2)
-                    gather_means(2)
-                if u == 2:
-                    fetch_means(3)
-                factors(u, 0)
-                factor_inverse(u, 1)
-                if u == 1:
-                    add_head(2, 2)
-                factors(u, 1)
-                if u == 1:
-                    add_head(2, 3)
-                    fetch_means(2)
-                quantise_weights(u)
-            if u >= 2:
-                for m in {2: [0,1], 3: [2,3]}[u]:
-                    residual(0, m)
-                    multiply(0, m)
-                for m in {2: [0,1], 3: [2,3]}[u]:
-                    finish(0, m)
+            if u == 1:
+                regroup(0)
+                factor_denominator(1, 0)
+                quantise_stream(0)
+                factor_inverse(1, 0)
+                factor_denominator(1, 1)
+                spread_means(2)
+                gather_means(2)
+                factors(1, 0)
+                factor_inverse(1, 1)
+                add_head(2, 2)
+                factors(1, 1)
+                add_head(2, 3)
+                fetch_means(2)
+                copy_weights(2)
+                quantise_weights(1)
+            if u == 2:
+                regroup(1)
+                quantise_stream(1)
+                factor_denominator(2, 0)
+                factor_inverse(2, 0)
+                factor_denominator(2, 1)
+                fetch_means(3)
+                factors(2, 0)
+                factor_inverse(2, 1)
+                copy_weights(4)
+                factors(2, 1)
+                residual(0, 0)
+                quantise_weights(2)
+                residual(0, 1)
+                multiply(0, 0)
+                multiply(0, 1)
+                finish(0, 0)
+                finish(0, 1)
+            if u == 3:
+                regroup(2)
+                residual(0, 2)
+                residual(0, 3)
+                multiply(0, 2)
+                multiply(0, 3)
+                factor_denominator(3, 0)
+                quantise_stream(2)
+                factor_inverse(3, 0)
+                factor_denominator(3, 1)
+                factors(3, 0)
+                factor_inverse(3, 1)
+                copy_weights(6)
+                factors(3, 1)
+                finish(0, 2)
+                quantise_weights(3)
+                finish(0, 3)
             for t in range(PACK):
                 scale_slot(u, t)
                 if u + 1 < PASSES:
                     transpose_slot(u + 1, t)
         regroup(3)
-        for m in [4,5,6,7]:
+        for m in (4, 5, 6, 7):
             residual(0, m)
             multiply(0, m)
         finish(0, 4)
         finish(0, 5)
         quantise_stream(3)
         open_late_bias()
-        finish(0, 6)
-        finish(0, 7)
         for m in range(ROW_TILES):
             residual(1, m)
+        finish(0, 6)
+        finish(0, 7)
         for m in range(3):
             multiply(1, m)
         for m in range(ROW_TILES):

@@ -110,9 +110,9 @@ def tile_axialattentionblock_pb_kernel(tc, xx, xy, x, norm2_w, out_w, out_b, gam
         load_weights(0)
         load_pair(2, False)
         load_pair(3, False)
+        load_weights(1)
         load_pair(4, False)
         load_pair(5, False)
-        load_weights(1)
         load_pass(3)
         load_weights(2)
         load_residual(0)
@@ -146,6 +146,11 @@ def tile_axialattentionblock_pb_kernel(tc, xx, xy, x, norm2_w, out_w, out_b, gam
         def slot_columns(name, u, r, t):
             return streams[(name, u)][:, r].rearrange("i n c -> i (n c)")[:, t::PACK]
 
+        def warm_up(n):
+            for i in range(n):
+                t = ps_weights.tile([P, POSITIONS], F32, name="warm_ps", tag="w_ps")
+                nc.tensor.matmul(t[:], lhsT=ident_bf[:], rhs=ident_bf[:].unsqueeze(1).to_broadcast([P, CHUNKS, P]), start=True, stop=True)
+
         def sum_positions(u):
             if u in ADDED_ON_TENSOR:
                 t = ps_products.tile([P, PACK, MEAN_COLUMNS], F32, name="mean_ps", tag="products")
@@ -163,6 +168,8 @@ def tile_axialattentionblock_pb_kernel(tc, xx, xy, x, norm2_w, out_w, out_b, gam
                 for i, block in enumerate(blocks):
                     nc.tensor.matmul(t[:, n, :], lhsT=block, rhs=minus_mean_weight[:],
                                      start=(i == 0), stop=(i == len(blocks) - 1))
+                if u == 0:
+                    warm_up([0,0,0,0][n])
             head_mean[u] = t
 
         def add_head(u, n):
@@ -359,12 +366,13 @@ def tile_axialattentionblock_pb_kernel(tc, xx, xy, x, norm2_w, out_w, out_b, gam
         add_head(1, 1)
 
         for u in range(PASSES):
-            if u != 0 and u + 1 < PASSES:
-                sum_positions(u + 1)
-            transpose_weights(2 * u)
-            transpose_weights(2 * u + 1)
             if u == 0:
-                sum_positions(1)
+                transpose_weights(0)
+            transpose_weights(2 * u + 1)
+            if u + 1 < PASSES:
+                sum_positions(u + 1)
+            if u > 0:
+                transpose_weights(2 * u)
             square_slot(u, 0)
             square_slot(u, 1)
             square_slot(u, 2)
@@ -377,15 +385,15 @@ def tile_axialattentionblock_pb_kernel(tc, xx, xy, x, norm2_w, out_w, out_b, gam
                 copy_weights(0)
                 factor_inverse(0, 0)
                 factor_denominator(0, 1)
-                spread_means(1)
-                gather_means(1)
                 factors(0, 0)
                 factor_inverse(0, 1)
                 add_head(1, 2)
                 factors(0, 1)
+                spread_means(1)
+                gather_means(1)
                 add_head(1, 3)
-                fetch_means(1)
                 quantise_weights(0)
+                fetch_means(1)
                 add_head(2, 0)
                 add_head(2, 1)
             if u == 1:
@@ -394,15 +402,15 @@ def tile_axialattentionblock_pb_kernel(tc, xx, xy, x, norm2_w, out_w, out_b, gam
                 quantise_stream(0)
                 factor_inverse(1, 0)
                 factor_denominator(1, 1)
-                spread_means(2)
-                gather_means(2)
                 factors(1, 0)
                 factor_inverse(1, 1)
                 add_head(2, 2)
                 factors(1, 1)
+                spread_means(2)
+                gather_means(2)
                 add_head(2, 3)
-                fetch_means(2)
                 copy_weights(2)
+                fetch_means(2)
                 quantise_weights(1)
             if u == 2:
                 regroup(1)
@@ -410,12 +418,12 @@ def tile_axialattentionblock_pb_kernel(tc, xx, xy, x, norm2_w, out_w, out_b, gam
                 factor_denominator(2, 0)
                 factor_inverse(2, 0)
                 factor_denominator(2, 1)
-                fetch_means(3)
                 factors(2, 0)
                 factor_inverse(2, 1)
-                copy_weights(4)
-                factors(2, 1)
                 residual(0, 0)
+                factors(2, 1)
+                fetch_means(3)
+                copy_weights(4)
                 quantise_weights(2)
                 residual(0, 1)
                 multiply(0, 0)

from contextlib import ExitStack

import concourse.mybir as mybir
from concourse.masks import make_identity

FLOPS = 2 * 1024 * 1024 * 1024

F32 = mybir.dt.float32
BF16 = mybir.dt.bfloat16
U32 = mybir.dt.uint32
U8 = mybir.dt.uint8
FP8X4 = mybir.dt.float8_e4m3fn_x4
ACT = mybir.ActivationFunctionType
ALU = mybir.AluOpType
AXIS = mybir.AxisListType

P = 128
POSITIONS = 512
CHUNKS = 4
HEADS = 4
QUADS = 32
PACK = 4
PASSES = 4
ROW_TILES = 8
ADDED_ON_TENSOR = (3,)
W_V = (0, 2, 4, 6)
RES_V = ((0, 0), (0, 1), (0, 2), (0, 3), (0, 4), (0, 5))
RES_G = ()
MEAN_COLUMNS = 2


def tile_axialattentionblock_pb_kernel(tc, xx, xy, x, norm2_w, out_w, out_b, gamma_att, out):
    nc = tc.nc
    with ExitStack() as ctx:
        const = ctx.enter_context(tc.tile_pool(name="const", bufs=1))
        inputs = ctx.enter_context(tc.tile_pool(name="inputs", bufs=1))
        keep = ctx.enter_context(tc.tile_pool(name="keep", bufs=1))
        sums = ctx.enter_context(tc.tile_pool(name="sums", bufs=3))
        stage = ctx.enter_context(tc.tile_pool(name="stage", bufs=2))
        small = ctx.enter_context(tc.tile_pool(name="small", bufs=4))
        ps_heads = ctx.enter_context(tc.psum_pool(name="ps_heads", bufs=4))
        ps_weights = ctx.enter_context(tc.psum_pool(name="ps_weights", bufs=2))
        ps_products = ctx.enter_context(tc.psum_pool(name="ps_products", bufs=2))
        ctx.enter_context(tc.manual_schedule())

        weight_bf = const.tile([P, 2, PACK], BF16, name="weight_bf")
        gamma_bf = const.tile([P, ROW_TILES], BF16, name="gamma_bf")
        bias_bf = const.tile([P, ROW_TILES], BF16, name="bias_bf")

        streams = {}
        xx_sb = {}
        xy_sb = {}
        w_sb = []
        x_sb = []

        def load_pair(k, by_head):
            b, n0 = k // 4, 2 * (k % 4)
            tiles = []
            for name, tiles_of in (("xx", xx_sb), ("xy", xy_sb)):
                t = inputs.tile([P, 2, POSITIONS], BF16, name="%s_%d" % (name, k))
                tiles_of[k] = t
                tiles.append(t)
            if by_head:
                for j in range(2):
                    for src, t in zip((xx, xy), tiles):
                        nc.sync.dma_start(
                            out=t[:, j, :], in_=src[b, n0 + j].rearrange("h (q r) c -> (h q) (r c)", r=CHUNKS))
            else:
                for src, t in zip((xx, xy), tiles):
                    nc.sync.dma_start(
                        out=t[:], in_=src[b, n0:n0 + 2].rearrange("n h (q r) c -> (h q) n (r c)", r=CHUNKS))

        def load_pass(u):
            b, n0 = u // 2, 4 * (u % 2)
            for name, src in (("xx", xx), ("xy", xy)):
                t = inputs.tile([P, CHUNKS, HEADS, P], BF16, name="%s_pass%d" % (name, u))
                streams[(name, u)] = t
            for n in range(HEADS):
                for name, src in (("xx", xx), ("xy", xy)):
                    nc.sync.dma_start(out=streams[(name, u)][:, :, n, :],
                                      in_=src[b, n0 + n].rearrange("h (q r) c -> (h q) r c", r=CHUNKS))

        def load_weights(i):
            t = inputs.tile([P, 2, 1024], BF16, name="w_sb%d" % i)
            nc.sync.dma_start(out=t[:], in_=out_w.rearrange("(p m) j -> p m j", m=ROW_TILES)[:, 2 * i:2 * i + 2, :])
            w_sb.append(t)

        def load_residual(b):
            t = inputs.tile([P, ROW_TILES, POSITIONS], BF16, name="x_sb%d" % b)
            nc.sync.dma_start(out=t[:], in_=x[b].rearrange("(p m) h w -> p m (h w)", m=ROW_TILES))
            x_sb.append(t)

        one = const.tile([P, 1], F32, name="one")
        nc.vector.memset(one[:], 1.0)
        warm = const.tile([P, 1], F32, name="warm")
        nc.scalar.activation(out=warm[:], in_=one[:], func=ACT.Sqrt)
        minus_mean_weight = const.tile([P, MEAN_COLUMNS], BF16, name="minus_mean_weight")
        nc.vector.memset(minus_mean_weight[:], -1.0 / POSITIONS)
        ident = const.tile([P, P], F32, name="ident")
        make_identity(nc, ident[:])
        ident_bf = const.tile([P, P], BF16, name="ident_bf")
        nc.vector.tensor_copy(out=ident_bf[:], in_=ident[:])

        load_pair(0, True)
        load_pair(1, True)
        with nc.allow_non_contiguous_dma(reason="three vectors of 1,024 values, eight values to a partition"):
            nc.sync.dma_start(out=weight_bf[:], in_=norm2_w.rearrange("(g p t) -> p g t", g=2, t=PACK))
            nc.sync.dma_start(out=gamma_bf[:], in_=gamma_att.rearrange("(p m) -> p m", m=ROW_TILES))
            nc.sync.dma_start(out=bias_bf[:], in_=out_b.rearrange("(p m) -> p m", m=ROW_TILES))
        load_weights(0)
        load_pair(2, False)
        load_pair(3, False)
        load_weights(1)
        load_pair(4, False)
        load_pair(5, False)
        load_pass(3)
        load_weights(2)
        load_residual(0)
        load_weights(3)
        load_residual(1)

        same_quad = const.tile([P, QUADS], F32, name="same_quad")
        nc.vector.tensor_reduce(out=same_quad[:], in_=ident[:].rearrange("c (q t) -> c q t", t=PACK), axis=AXIS.X, op=ALU.add)
        same_slot = const.tile([P, PACK], F32, name="same_slot")
        nc.vector.tensor_reduce(out=same_slot[:], in_=ident[:].rearrange("c (q t) -> c t q", t=PACK), axis=AXIS.X, op=ALU.add)
        half_w = const.tile([P, 2, PACK], F32, name="half_w")
        gamma = const.tile([P, ROW_TILES], F32, name="gamma")
        gamma_bias = const.tile([P, ROW_TILES], F32, name="gamma_bias")

        head_mean = {}
        spread_mean = {}
        moved_mean = {}
        minus_mean = {}
        summed = {}
        slot_ps = {}
        square_sum = {}
        deviation = {}
        denominator = {}
        inverse = {}
        factor = {}
        scaled = {}
        grouped = {}
        g_codes = {}
        g_scales = {}

        def slot_columns(name, u, r, t):
            return streams[(name, u)][:, r].rearrange("i n c -> i (n c)")[:, t::PACK]

        def warm_up(n):
            for i in range(n):
                t = ps_weights.tile([P, POSITIONS], F32, name="warm_ps", tag="w_ps")
                nc.tensor.matmul(t[:], lhsT=ident_bf[:], rhs=ident_bf[:].unsqueeze(1).to_broadcast([P, CHUNKS, P]), start=True, stop=True)

        def sum_positions(u):
            if u in ADDED_ON_TENSOR:
                t = ps_products.tile([P, PACK, MEAN_COLUMNS], F32, name="mean_ps", tag="products")
                for slot in range(PACK):
                    blocks = [slot_columns(name, u, r, slot) for name in ("xx", "xy") for r in range(CHUNKS)]
                    for i, block in enumerate(blocks):
                        nc.tensor.matmul(t[:, slot, :], lhsT=block, rhs=minus_mean_weight[:],
                                         start=(i == 0), stop=(i == len(blocks) - 1))
                moved_mean[u] = t
                return
            t = ps_products.tile([P, HEADS, MEAN_COLUMNS], F32, name="mean_ps", tag="products")
            for n in range(HEADS):
                k, j = 2 * u + n // 2, n % 2
                blocks = [src[k][:, j, P * r:P * r + P] for src in (xx_sb, xy_sb) for r in range(CHUNKS)]
                for i, block in enumerate(blocks):
                    nc.tensor.matmul(t[:, n, :], lhsT=block, rhs=minus_mean_weight[:],
                                     start=(i == 0), stop=(i == len(blocks) - 1))
                if u == 0:
                    warm_up([0,0,0,0][n])
            head_mean[u] = t

        def add_head(u, n):
            if n == 0:
                fresh = sums.tile([P, CHUNKS, PACK, HEADS, QUADS], F32, name="summed")
                summed[u] = fresh
            k, j = 2 * u + n // 2, n % 2
            a, b = [src[k][:, j, :].rearrange("p (r q t) -> p r t q", r=CHUNKS, t=PACK) for src in (xx_sb, xy_sb)]
            nc.vector.tensor_tensor(out=summed[u][:, :, :, n, :], in0=a, in1=b, op=ALU.add)

        def spread_means(u):
            spread = small.tile([P, HEADS, QUADS], F32, name="spread")
            spread_mean[u] = spread
            nc.vector.tensor_tensor(
                out=spread[:], in0=same_quad[:].unsqueeze(1).to_broadcast([P, HEADS, QUADS]),
                in1=head_mean[u][:, :, 0:1].to_broadcast([P, HEADS, QUADS]), op=ALU.mult)

        def gather_means(u):
            moved = ps_products.tile([P, PACK, 1], F32, name="moved", tag="products")
            moved_mean[u] = moved
            nc.tensor.matmul(moved[:, :, 0], lhsT=spread_mean[u][:].rearrange("p n q -> p (n q)"), rhs=same_slot[:], start=True, stop=True)

        def fetch_means(u):
            t = small.tile([P, PACK], F32, name="minus_mean")
            nc.vector.tensor_copy(out=t[:], in_=moved_mean[u][:, :, 0])
            minus_mean[u] = t

        def transpose_slot(u, t):
            bank = ps_heads.tile([P, POSITIONS], F32, name="slot_ps", tag="heads")
            for r in range(CHUNKS):
                cols = slice(P * r, P * r + P)
                if u in ADDED_ON_TENSOR:
                    nc.tensor.matmul(bank[:, cols], lhsT=slot_columns("xx", u, r, t), rhs=ident_bf[:], start=True, stop=False)
                    nc.tensor.matmul(bank[:, cols], lhsT=slot_columns("xy", u, r, t), rhs=ident_bf[:], start=False, stop=True)
                    continue
                nc.tensor.transpose(bank[:, P * r:P * r + P], summed[u][:, r, t, :, :].rearrange("p n q -> p (n q)"), ident[:])
            slot_ps[(u, t)] = bank

        def square_slot(u, t):
            if t % 2 == 0:
                fresh = small.tile([P, 2], F32, name="square_sum")
                square_sum[(u, t // 2)] = fresh
            unused = small.tile([P, POSITIONS], BF16, name="unused")
            nc.scalar.activation(out=unused[:], in_=slot_ps[(u, t)][:], func=ACT.Square, bias=minus_mean[u][:, t:t + 1],
                                 scale=1.0, accum_out=square_sum[(u, t // 2)][:, t % 2:t % 2 + 1])

        def deviations(u, i):
            d = small.tile([P, 2], F32, name="deviation")
            nc.scalar.activation(out=d[:], in_=square_sum[(u, i)][:], func=ACT.Sqrt, scale=1.0 / (4.0 * (POSITIONS - 1)))
            deviation[(u, i)] = d

        def factor_denominator(u, i):
            d = small.tile([P, 2], F32, name="denominator")
            nc.vector.tensor_scalar(out=d[:], in0=deviation[(u, i)][:], scalar1=1e-8, scalar2=None, op0=ALU.add)
            denominator[(u, i)] = d

        def factor_inverse(u, i):
            d = small.tile([P, 2], F32, name="inverse")
            nc.vector.reciprocal(out=d[:], in_=denominator[(u, i)][:])
            inverse[(u, i)] = d

        def factors(u, i):
            f = small.tile([P, 2], F32, name="factor")
            nc.vector.tensor_tensor(out=f[:], in0=inverse[(u, i)][:], in1=half_w[:, u % 2, 2 * i:2 * i + 2], op=ALU.mult)
            factor[(u, i)] = f

        def scale_slot(u, t):
            if t == 0:
                fresh = stage.tile([P, PACK, POSITIONS], BF16, name="scaled")
                scaled[u] = fresh
            nc.scalar.activation(
                out=scaled[u][:, t, :].rearrange("c (p r) -> c p r", r=CHUNKS),
                in_=slot_ps[(u, t)][:].rearrange("c (r p) -> c p r", r=CHUNKS),
                func=ACT.Copy, scale=factor[(u, t // 2)][:, t % 2:t % 2 + 1])

        def regroup(u):
            t = stage.tile([P, POSITIONS, PACK], BF16, name="grouped", align_bytes=64)
            dst = t[:].rearrange("p (c i) t -> p c t i", i=4)
            src = scaled[u][:].rearrange("p t (c i) -> p c t i", i=4)
            if u == 3 and True:
                k = 84
                nc.vector.tensor_copy(out=dst[:, :k], in_=src[:, :k])
                nc.scalar.copy(out=dst[:, k:], in_=src[:, k:])
            else:
                nc.vector.tensor_copy(out=dst, in_=src)
            grouped[u] = t

        def quantise_stream(u):
            codes = keep.tile([P, POSITIONS], U32, name="g_codes%d" % u, align_bytes=64)
            scales = keep.tile([P, POSITIONS], U8, name="g_scales%d" % u, align_bytes=64)
            nc.vector.quantize_mx(out=codes[:].bitcast(FP8X4), scales=scales[:],
                                  in_=grouped[u][:].rearrange("p w t -> p (w t)"))
            g_codes[u] = codes
            g_scales[u] = scales

        w_ps = {}
        w_grouped = {}
        w_codes = {}
        w_scales = {}

        def transpose_weights(m):
            bank = ps_weights.tile([P, 2, 2, P], F32, name="w_ps", tag="w_ps")
            words = w_sb[m // 2][:, m % 2, :].bitcast(F32)
            for g in range(2):
                for h in range(2):
                    nc.tensor.transpose(bank[:, g, h, :], words[:, 256 * g + h:256 * g + 256:2], ident[:])
            w_ps[m] = bank

        def copy_weights(m):
            i = m % 2
            if m // 2 not in w_grouped:
                fresh = stage.tile([P, 2, 2, P, PACK], BF16, name="w_grouped", align_bytes=64)
                w_grouped[m // 2] = fresh
            dst = w_grouped[m // 2][:, i].bitcast(F32)
            src = w_ps[m][:].rearrange("p g h o -> p g o h")
            if m in W_V:
                nc.vector.tensor_copy(out=dst, in_=src)
            else:
                nc.scalar.copy(out=dst, in_=src)

        def quantise_weights(i):
            codes = keep.tile([P, 4, P], U32, name="w_codes%d" % i, align_bytes=64)
            scales = keep.tile([P, 4, P], U8, name="w_scales%d" % i, align_bytes=64)
            nc.vector.quantize_mx(out=codes[:].rearrange("p a o -> p (a o)").bitcast(FP8X4),
                                  scales=scales[:].rearrange("p a o -> p (a o)"),
                                  in_=w_grouped[i][:].rearrange("p i g o t -> p (i g o t)"))
            w_codes[i] = codes
            w_scales[i] = scales

        result = {}
        product = {}

        def residual(b, m):
            if m % 2 == 0:
                fresh = keep.tile([P, 2, POSITIONS], F32, name="result%d%d" % (b, m // 2))
                result[(b, m // 2)] = fresh
            dst = result[(b, m // 2)][:, m % 2, :]
            if (b, m) in RES_V:
                nc.vector.tensor_scalar(out=dst, in0=x_sb[b][:, m, :], scalar1=1.0, scalar2=gamma_bias[:, m:m + 1],
                                        op0=ALU.mult, op1=ALU.add)
            elif (b, m) in RES_G:
                nc.gpsimd.tensor_scalar(out=dst, in0=x_sb[b][:, m, :], scalar1=1.0, scalar2=(gamma_bias if b == 0 else late_bias[0])[:, m:m + 1],
                                        op0=ALU.mult, op1=ALU.add)
            else:
                nc.scalar.activation(out=dst, in_=x_sb[b][:, m, :], func=ACT.Identity,
                                     bias=gamma_bias[:, m:m + 1], scale=1.0)

        late_bias = []

        def open_late_bias():
            t = const.tile([P, ROW_TILES], F32, name="late_bias")
            nc.vector.tensor_copy(out=t[:], in_=gamma_bias[:])
            late_bias.append(t)

        def multiply(b, m):
            if b == 0 and m < 6:
                t = ps_products.tile([P, POSITIONS], F32, name="product", tag="products")
            elif b == 0:
                t = ps_weights.tile([P, POSITIONS], F32, name="product", tag="w_ps")
            else:
                t = ps_heads.tile([P, POSITIONS], F32, name="product", tag="heads")
            for g in range(2):
                nc.tensor.matmul_mx(
                    out=t[:],
                    lhsT=w_codes[m // 2][:, 2 * (m % 2) + g, :].bitcast(FP8X4),
                    lhsT_scale=w_scales[m // 2][:, 2 * (m % 2) + g, :],
                    rhs=g_codes[2 * b + g][:].bitcast(FP8X4),
                    rhs_scale=g_scales[2 * b + g][:],
                    start=(g == 0), stop=(g == 1))
            product[(b, m)] = t

        def finish(b, m):
            t = result[(b, m // 2)]
            nc.vector.scalar_tensor_tensor(out=t[:, m % 2, :], in0=product[(b, m)][:], scalar=gamma[:, m:m + 1],
                                           in1=t[:, m % 2, :], op0=ALU.mult, op1=ALU.add)
            view = out[b].rearrange("(p m) h w -> p m (h w)", m=ROW_TILES)
            if b == 1 or m >= 4:
                nc.sync.dma_start(out=view[:, m, :], in_=t[:, m % 2, :])
            elif m % 2 == 1:
                nc.sync.dma_start(out=view[:, m - 1:m + 1, :], in_=t[:])

        sum_positions(0)
        for n in range(HEADS):
            add_head(0, n)
        spread_means(0)
        gather_means(0)
        for t in range(PACK):
            transpose_slot(0, t)
        fetch_means(0)
        nc.vector.tensor_scalar(out=half_w[:], in0=weight_bf[:], scalar1=0.5, scalar2=None, op0=ALU.mult)
        nc.vector.tensor_copy(out=gamma[:], in_=gamma_bf[:])
        nc.vector.tensor_tensor(out=gamma_bias[:], in0=gamma_bf[:], in1=bias_bf[:], op=ALU.mult)
        add_head(1, 0)
        add_head(1, 1)

        for u in range(PASSES):
            if u == 0:
                transpose_weights(0)
            transpose_weights(2 * u + 1)
            if u + 1 < PASSES:
                sum_positions(u + 1)
            if u > 0:
                transpose_weights(2 * u)
            square_slot(u, 0)
            square_slot(u, 1)
            square_slot(u, 2)
            deviations(u, 0)
            square_slot(u, 3)
            deviations(u, 1)
            copy_weights(2 * u + 1)
            if u == 0:
                factor_denominator(0, 0)
                copy_weights(0)
                factor_inverse(0, 0)
                factor_denominator(0, 1)
                factors(0, 0)
                factor_inverse(0, 1)
                add_head(1, 2)
                factors(0, 1)
                spread_means(1)
                gather_means(1)
                add_head(1, 3)
                quantise_weights(0)
                fetch_means(1)
                add_head(2, 0)
                add_head(2, 1)
            if u == 1:
                regroup(0)
                factor_denominator(1, 0)
                quantise_stream(0)
                factor_inverse(1, 0)
                factor_denominator(1, 1)
                factors(1, 0)
                factor_inverse(1, 1)
                add_head(2, 2)
                factors(1, 1)
                spread_means(2)
                gather_means(2)
                add_head(2, 3)
                copy_weights(2)
                fetch_means(2)
                quantise_weights(1)
            if u == 2:
                regroup(1)
                quantise_stream(1)
                factor_denominator(2, 0)
                factor_inverse(2, 0)
                factor_denominator(2, 1)
                factors(2, 0)
                factor_inverse(2, 1)
                residual(0, 0)
                factors(2, 1)
                fetch_means(3)
                copy_weights(4)
                quantise_weights(2)
                residual(0, 1)
                multiply(0, 0)
                multiply(0, 1)
                finish(0, 0)
                finish(0, 1)
            if u == 3:
                regroup(2)
                residual(0, 2)
                residual(0, 3)
                multiply(0, 2)
                multiply(0, 3)
                factor_denominator(3, 0)
                quantise_stream(2)
                factor_inverse(3, 0)
                factor_denominator(3, 1)
                factors(3, 0)
                factor_inverse(3, 1)
                copy_weights(6)
                factors(3, 1)
                finish(0, 2)
                quantise_weights(3)
                finish(0, 3)
            for t in range(PACK):
                scale_slot(u, t)
                if u + 1 < PASSES:
                    transpose_slot(u + 1, t)
        regroup(3)
        for m in (4, 5, 6, 7):
            residual(0, m)
            multiply(0, m)
        finish(0, 4)
        finish(0, 5)
        quantise_stream(3)
        open_late_bias()
        for m in range(ROW_TILES):
            residual(1, m)
        finish(0, 6)
        finish(0, 7)
        for m in range(3):
            multiply(1, m)
        for m in range(ROW_TILES):
            finish(1, m)
            if m + 3 < ROW_TILES:
                multiply(1, m + 3)
